import numpy as np
import ml_dtypes


def mxq(x, axis, fmt="e4m3"):
    dtype, down = {"e4m3": (ml_dtypes.float8_e4m3fn, 7), "e5m2": (ml_dtypes.float8_e5m2, 14)}[fmt]
    v = np.moveaxis(np.asarray(x, np.float32).astype(ml_dtypes.bfloat16).astype(np.float64), axis, -1)
    blocks = v.reshape(v.shape[:-1] + (-1, 32))
    amax = np.abs(blocks).max(-1, keepdims=True)
    byte = np.maximum(np.where(amax > 0, np.frexp(amax)[1] - 1 + 127, 0) - down, 1)
    scale = np.exp2(byte - 127.0)
    codes = (blocks / scale).astype(np.float32).astype(dtype).astype(np.float64)
    return np.moveaxis((codes * scale).reshape(v.shape), -1, axis)


WIDE = False


def mx_kscale(k):
    if not WIDE:
        return np.ones(k)
    levels = np.array([10, -10, 5, -5, 0])
    if k % 512:
        return np.exp2(np.random.permutation(np.resize(levels, k // 32))).repeat(32)
    a = np.empty((k // 512, 16))
    for p in range(k // 512):
        a[p, :8] = np.random.permutation(np.resize(levels, 8))
        for g in range(8):
            far = levels[np.abs(levels - a[p, g]) >= 10]
            a[p, g + 8] = far[np.random.randint(len(far))]
    return np.exp2(a.ravel()).repeat(32)


BF16 = ml_dtypes.bfloat16


def bf(x):
    return np.asarray(x, np.float32).astype(BF16)


def f64(x):
    return np.asarray(x).astype(np.float64)


B, L, E, H, HD, F, G = 4, 128, 1024, 8, 128, 2048, 2048
EPS = 1e-6


def rmsnorm(x, g):
    return x * (1.0 / np.sqrt(np.mean(x * x, axis=-1, keepdims=True) + EPS)) * g


def rope_diag():
    pair = np.arange(HD) // 2
    theta = 10000.0 ** (-2.0 * pair / HD)
    return np.cos(np.arange(L)[:, None] * theta[None, :])


def setup_inputs():
    s = mx_kscale(E)
    return {"x": bf(np.random.standard_normal((B, L, E))),
            "g": bf((1.0 + 0.1 * np.random.standard_normal(E)) * s),
            "wq": bf(np.random.standard_normal((E, H * HD)) / np.sqrt(E) / s[:, None]),
            "wk": bf(np.random.standard_normal((E, H * HD)) / np.sqrt(E) / s[:, None])}


def reference(x, g, wq, wk):
    hq = mxq(rmsnorm(f64(x), f64(g)), 2, "e4m3")
    c = rope_diag()
    q = (hq @ mxq(f64(wq), 0, "e4m3")).reshape(B, L, H, HD).transpose(0, 2, 1, 3) * c
    k = (hq @ mxq(f64(wk), 0, "e4m3")).reshape(B, L, H, HD).transpose(0, 2, 1, 3) * c
    return q, k

@@ -1,0 +1,322 @@
+import math
+from contextlib import ExitStack
+
+import concourse.mybir as mybir
+
+FP8X4 = mybir.dt.float8_e4m3fn_x4
+BF16 = mybir.dt.bfloat16
+F32 = mybir.dt.float32
+I32 = mybir.dt.int32
+U32 = mybir.dt.uint32
+U8 = mybir.dt.uint8
+ALU = mybir.AluOpType
+ACT = mybir.ActivationFunctionType
+
+P = 128
+B, L, E, H, HD = 4, 128, 1024, 8, 128
+EPS = 1e-6
+FLOPS = 2 * B * L * E * 2 * H * HD
+NT = 4
+NG = 2
+TURN = 1.0 / (2.0 * math.pi)
+CHUNKS = [(0, 0, 512), (0, 512, 512), (1, 0, 512), (1, 512, 256), (1, 768, 256)]
+VCOLS = {(0, 0): 256, (0, 1): 256, (1, 0): 256}
+GCOLS = {(0, 1): 256, (2, 0): 256, (3, 0): 256, (4, 0): 256}
+SPLIT_STATS = [True, True, False, False]
+
+
+def tile_llamaselfattentionblock_pa_kernel(tc, x, g, wq, wk, out_0, out_1):
+    nc = tc.nc
+    nch = len(CHUNKS)
+    with ExitStack() as ctx:
+        const = ctx.enter_context(tc.tile_pool(name="const", bufs=1))
+        psum = ctx.enter_context(tc.psum_pool(name="psum", bufs=8))
+        ctx.enter_context(tc.manual_schedule())
+
+        grow = const.tile([P, E], BF16)
+        nc.vector.memset(grow[:], 0.0)
+        xv = x.rearrange("b l k -> (b l) k").rearrange("(p j) k -> p j k", j=NT)
+        xt = []
+        for j in range(NT):
+            xj = const.tile([P, E], BF16, name="x%d" % j)
+            nc.sync.dma_start(out=xj[:], in_=xv[:, j, :])
+            xt.append(xj)
+            if j == 0:
+                nc.sync.dma_start(out=grow[0:1, :], in_=g.rearrange("(o k) -> o k", o=1))
+        wr = []
+        for c in range(nch):
+            m, n0, wd = CHUNKS[c]
+            w = wq if m == 0 else wk
+            wt = const.tile([P, NG, 4, wd], BF16, name="wr%d" % c)
+            for gg in range(NG):
+                nc.sync.dma_start(
+                    out=wt[:, gg, :, :],
+                    in_=w[512 * gg : 512 * gg + 512, n0 : n0 + wd].rearrange("(p t) n -> p t n", p=P),
+                )
+            wr.append(wt)
+
+        ones = const.tile([P, P], BF16)
+        nc.gpsimd.memset(ones[:], 1.0)
+        neghalf = const.tile([P, 1], F32)
+        nc.gpsimd.memset(neghalf[:], -0.5)
+        warm = const.tile([P, 1], F32)
+        nc.scalar.activation(out=warm[:], in_=neghalf[:], func=ACT.Sin)
+        pj = const.tile([P, NT], I32)
+        nc.gpsimd.iota(pj[:], pattern=[[0, NT]], base=0, channel_multiplier=1)
+        jj = const.tile([P, NT], I32)
+        nc.gpsimd.iota(jj[:], pattern=[[1, NT]], base=0, channel_multiplier=0)
+        pdiff = const.tile([P, 32, B], F32)
+        nc.gpsimd.iota(
+            pdiff[:], pattern=[[1, 32], [32, B]], base=0, channel_multiplier=-1, allow_small_or_imprecise_dtypes=True
+        )
+        perm = const.tile([P, P], BF16)
+        nc.gpsimd.tensor_scalar(
+            out=perm[:], in0=pdiff[:].rearrange("p l b -> p (l b)"), scalar1=0.0, scalar2=None, op0=ALU.is_equal
+        )
+
+        th = const.tile([P, 64], F32)
+        nc.vector.memset(th[:, 0:1], 1.0)
+        ratio = 10000.0 ** (-1.0 / 64.0)
+        for s in range(6):
+            wd = 1 << s
+            nc.vector.tensor_scalar(
+                out=th[:, wd : 2 * wd], in0=th[:, 0:wd], scalar1=ratio**wd, scalar2=None, op0=ALU.mult
+            )
+        l0i = const.tile([P, NT], I32)
+        nc.vector.tensor_scalar(out=l0i[:], in0=pj[:], scalar1=124, scalar2=None, op0=ALU.bitwise_and)
+        lji = const.tile([P, NT], I32)
+        nc.vector.tensor_tensor(out=lji[:], in0=l0i[:], in1=jj[:], op=ALU.bitwise_or)
+        ljt = const.tile([P, NT], F32)
+        nc.vector.tensor_scalar(out=ljt[:], in0=lji[:], scalar1=TURN, scalar2=None, op0=ALU.mult)
+        yy = const.tile([P, NT, 64], F32)
+        for j in range(NT):
+            nc.vector.tensor_scalar(
+                out=yy[:, j, :], in0=th[:], scalar1=ljt[:, j : j + 1], scalar2=0.25, op0=ALU.mult, op1=ALU.add
+            )
+
+        gp = psum.tile([P, E], BF16, tag="bank", name="gp")
+        for hf in range(2):
+            sl = slice(512 * hf, 512 * hf + 512)
+            nc.tensor.matmul(out=gp[:, sl], lhsT=ones[:], rhs=grow[:].rearrange("p (i t) -> p t i", t=4)[:, 2 * hf : 2 * hf + 2, :], start=True, stop=True)
+
+        rstds = []
+        for j in range(NT):
+            me = const.tile([P, 1], F32, name="me%d" % j)
+            msa = const.tile([P, 1], F32, name="msa%d" % j)
+            if SPLIT_STATS[j]:
+                junka = const.tile([P, 512], BF16, name="junka%d" % j)
+                nc.scalar.activation(
+                    out=junka[:], in_=xt[j][:, 0:512], func=ACT.Square, scale=1.0 / 32.0, accum_out=msa[:]
+                )
+                junkb = const.tile([P, 512], F32, name="junkb%d" % j)
+                msb = const.tile([P, 1], F32, name="msb%d" % j)
+                nc.vector.scalar_tensor_tensor(
+                    out=junkb[:],
+                    in0=xt[j][:, 512:1024],
+                    scalar=1.0 / 1024.0,
+                    in1=xt[j][:, 512:1024],
+                    op0=ALU.mult,
+                    op1=ALU.mult,
+                    accum_out=msb[:],
+                )
+                nc.gpsimd.tensor_scalar(
+                    out=me[:], in0=msa[:], scalar1=msb[:, 0:1], scalar2=EPS, op0=ALU.add, op1=ALU.add
+                )
+            else:
+                junka = const.tile([P, E], BF16, name="junka%d" % j)
+                nc.scalar.activation(out=junka[:], in_=xt[j][:], func=ACT.Square, scale=1.0 / 32.0, accum_out=msa[:])
+                nc.gpsimd.tensor_scalar(out=me[:], in0=msa[:], scalar1=1.0, scalar2=EPS, op0=ALU.mult, op1=ALU.add)
+            rstd = const.tile([P, 1], F32, name="rstd%d" % j)
+            nc.gpsimd.tensor_tensor(out=rstd[:], in0=me[:], in1=neghalf[:], op=ALU.pow)
+            rstds.append(rstd)
+
+        yi = const.tile([P, NT, 64], I32)
+        nc.vector.tensor_copy(out=yi[:], in_=yy[:])
+        yf = const.tile([P, NT, 64], F32)
+        nc.vector.tensor_copy(out=yf[:], in_=yi[:])
+        rr = const.tile([P, NT, 64], F32)
+        nc.vector.tensor_tensor(out=rr[:], in0=yy[:], in1=yf[:], op=ALU.subtract)
+        nr = const.tile([P, NT, 64], F32)
+        nc.vector.scalar_tensor_tensor(
+            out=nr[:], in0=rr[:], scalar=0.5, in1=rr[:], op0=ALU.is_gt, op1=ALU.subtract
+        )
+        ctab = const.tile([P, NT, 64, 2], F32)
+        nc.scalar.activation(
+            out=ctab[:],
+            in_=nr[:].unsqueeze(3).to_broadcast([P, NT, 64, 2]),
+            func=ACT.Sin,
+            scale=-2.0 * math.pi,
+        )
+
+        tps = []
+        for j in range(NT):
+            hj = const.tile([P, E], BF16, name="h%d" % j)
+            nc.vector.scalar_tensor_tensor(
+                out=hj[:].rearrange("p (t i) -> p t i", t=4),
+                in0=xt[j][:].rearrange("p (i t) -> p t i", t=4),
+                scalar=rstds[j][:, 0:1],
+                in1=gp[:].rearrange("p (t i) -> p t i", t=4),
+                op0=ALU.mult,
+                op1=ALU.mult,
+            )
+            tp = psum.tile([P, 8, P], BF16, tag="bank", name="tp%d" % j)
+            for q in range(8):
+                q0 = 256 * (q % 4) + P * (q // 4)
+                nc.tensor.transpose(out=tp[:, q, :], in_=hj[:, q0 : q0 + P], identity=perm[:])
+            tps.append(tp)
+
+        wgs = [const.tile([P, NG, CHUNKS[c][2], 4], BF16, name="wg%d" % c, align_bytes=64) for c in range(nch)]
+
+        def regroup(eng_copy, c, gg, c0, c1):
+            eng_copy(
+                out=wgs[c][:, gg, c0:c1, :].rearrange("p (c i) t -> p c t i", i=4),
+                in_=wr[c][:, gg, :, c0:c1].rearrange("p t (c i) -> p c t i", i=4),
+            )
+
+        def regroup_s(c, gg):
+            c1 = CHUNKS[c][2] - GCOLS.get((c, gg), 0)
+            if VCOLS.get((c, gg), 0) < c1:
+                regroup(nc.scalar.copy, c, gg, VCOLS.get((c, gg), 0), c1)
+
+        def regroup_g(c, gg, one):
+            c1 = CHUNKS[c][2]
+            for c0 in range(c1 - GCOLS[(c, gg)], c1, P):
+                nc.gpsimd.tensor_scalar(
+                    out=wgs[c][:, gg, c0 : c0 + P, :],
+                    in0=wr[c][:, gg, :, c0 : c0 + P].rearrange("p t n -> p n t"),
+                    scalar1=one,
+                    scalar2=0.0,
+                    op0=ALU.mult,
+                    op1=ALU.add,
+                )
+
+        def gate(k):
+            one = const.tile([P, 1], F32, name="one%d" % k)
+            nc.vector.memset(one[:], 1.0)
+            return one[:, 0:1]
+
+        def regroup_v(c, gg):
+            regroup(nc.vector.tensor_copy, c, gg, 0, VCOLS[(c, gg)])
+
+        regroup_g(0, 1, 1.0)
+        regroup_s(0, 0)
+        hgs = []
+        for j in range(NT):
+            hg = const.tile([P, NG, P, 4], BF16, name="hg%d" % j, align_bytes=64)
+            nc.scalar.copy(out=hg[:], in_=tps[j][:].rearrange("p (g t) l -> p g l t", t=4))
+            hgs.append(hg)
+        for c in range(nch):
+            for gg in range(NG):
+                if (c, gg) != (0, 0):
+                    regroup_s(c, gg)
+
+        hw = const.tile([P, NT, NG * P], U32, align_bytes=64)
+        hs = const.tile([P, NT, NG * P], U8, align_bytes=64)
+        wws = [const.tile([P, NG, CHUNKS[c][2]], U32, name="ww%d" % c, align_bytes=64) for c in range(nch)]
+        wss = [const.tile([P, NG, CHUNKS[c][2]], U8, name="ws%d" % c, align_bytes=64) for c in range(nch)]
+        accs = {}
+
+        def h_quant(j):
+            nc.vector.quantize_mx(
+                out=hw[:, j, :].bitcast(FP8X4),
+                scales=hs[:, j, :],
+                in_=hgs[j][:].rearrange("p g l t -> p (g l t)"),
+            )
+
+        def w_quant(c, gg):
+            nc.vector.quantize_mx(
+                out=wws[c][:, gg, :].bitcast(FP8X4),
+                scales=wss[c][:, gg, :],
+                in_=wgs[c][:, gg, :, :].rearrange("p n t -> p (n t)"),
+            )
+
+        def w_quant_both(c):
+            nc.vector.quantize_mx(
+                out=wws[c][:].rearrange("p g n -> p (g n)").bitcast(FP8X4),
+                scales=wss[c][:].rearrange("p g n -> p (g n)"),
+                in_=wgs[c][:].rearrange("p g n t -> p (g n t)"),
+            )
+
+        def one_pass(acc, c, j, gg):
+            nc.tensor.matmul_mx(
+                out=acc,
+                lhsT=hw[:, j, P * gg : P * gg + P].bitcast(FP8X4),
+                lhsT_scale=hs[:, j, P * gg : P * gg + P],
+                rhs=wws[c][:, gg, :].bitcast(FP8X4),
+                rhs_scale=wss[c][:, gg, :],
+                start=(gg == 0),
+                stop=(gg == NG - 1),
+            )
+
+        def passes_wide(c, gg):
+            if gg == 0:
+                accs[c] = [psum.tile([P, 512], F32, tag="bank", name="acc%d_%d" % (c, j)) for j in range(NT)]
+            for j in range(NT):
+                one_pass(accs[c][j][:], c, j, gg)
+
+        def passes_narrow(c):
+            accs[c] = [psum.tile([P, 2, 256], F32, tag="bank", name="acc%d_%d" % (c, jp)) for jp in range(2)]
+            for j in range(NT):
+                for gg in range(NG):
+                    one_pass(accs[c][j // 2][:, j % 2, :], c, j, gg)
+
+        def rope_store(c):
+            m, n0, wd = CHUNKS[c]
+            om = out_0 if m == 0 else out_1
+            nh = wd // HD
+            h0 = n0 // HD
+            osb = const.tile([P, nh, NT, HD], F32, name="osb%d" % c)
+            ct = ctab[:].rearrange("p j i e -> p j (i e)")
+            if wd == 512:
+                for j in range(NT):
+                    nc.vector.tensor_tensor(
+                        out=osb[:, :, j, :],
+                        in0=accs[c][j][:].rearrange("p (n d) -> p n d", d=HD),
+                        in1=ct[:, j, :].unsqueeze(1).to_broadcast([P, nh, HD]),
+                        op=ALU.mult,
+                    )
+            else:
+                for jp in range(2):
+                    nc.vector.tensor_tensor(
+                        out=osb[:, :, 2 * jp : 2 * jp + 2, :],
+                        in0=accs[c][jp][:].rearrange("p j (n d) -> p n j d", d=HD),
+                        in1=ct[:, 2 * jp : 2 * jp + 2, :].unsqueeze(1).to_broadcast([P, nh, 2, HD]),
+                        op=ALU.mult,
+                    )
+            for b in range(B):
+                nc.sync.dma_start(
+                    out=om[b, h0 : h0 + nh, :, :].rearrange("n (lh j) d -> lh n (j d)", j=NT),
+                    in_=osb[b:P:4, :, :, :].rearrange("p n j d -> p n (j d)"),
+                )
+
+        h_quant(0)
+        regroup_v(0, 0)
+        h_quant(1)
+        w_quant(0, 0)
+        h_quant(2)
+        regroup_v(0, 1)
+        h_quant(3)
+        regroup_v(1, 0)
+        passes_wide(0, 0)
+        w_quant(0, 1)
+        passes_wide(0, 1)
+        w_quant(1, 0)
+        passes_wide(1, 0)
+        regroup_g(2, 0, gate(0))
+        rope_store(0)
+        w_quant(1, 1)
+        passes_wide(1, 1)
+        w_quant(2, 0)
+        passes_wide(2, 0)
+        regroup_g(3, 0, gate(1))
+        rope_store(1)
+        w_quant(2, 1)
+        passes_wide(2, 1)
+        w_quant_both(3)
+        passes_narrow(3)
+        regroup_g(4, 0, gate(2))
+        rope_store(2)
+        w_quant_both(4)
+        passes_narrow(4)
+        rope_store(3)
+        rope_store(4)

@@ -20,9 +20,9 @@ NT = 4
 NG = 2
 TURN = 1.0 / (2.0 * math.pi)
 CHUNKS = [(0, 0, 512), (0, 512, 512), (1, 0, 512), (1, 512, 256), (1, 768, 256)]
-VCOLS = {(0, 0): 256, (0, 1): 256, (1, 0): 256}
+VCOLS = {(1, 0): 256}
 GCOLS = {(0, 1): 256, (2, 0): 256, (3, 0): 256, (4, 0): 256}
-SPLIT_STATS = [True, True, False, False]
+SPLIT_STATS = [True, True, True, False]
 
 
 def tile_llamaselfattentionblock_pa_kernel(tc, x, g, wq, wk, out_0, out_1):
@@ -33,8 +33,9 @@ def tile_llamaselfattentionblock_pa_kernel(tc, x, g, wq, wk, out_0, out_1):
         psum = ctx.enter_context(tc.psum_pool(name="psum", bufs=8))
         ctx.enter_context(tc.manual_schedule())
 
-        grow = const.tile([P, E], BF16)
-        nc.vector.memset(grow[:], 0.0)
+        gwords = const.tile([P, E // 2], I32, name="gwords")
+        nc.gpsimd.memset(gwords[:], 0)
+        grow = gwords[:].bitcast(BF16)
         xv = x.rearrange("b l k -> (b l) k").rearrange("(p j) k -> p j k", j=NT)
         xt = []
         for j in range(NT):
@@ -42,7 +43,7 @@ def tile_llamaselfattentionblock_pa_kernel(tc, x, g, wq, wk, out_0, out_1):
             nc.sync.dma_start(out=xj[:], in_=xv[:, j, :])
             xt.append(xj)
             if j == 0:
-                nc.sync.dma_start(out=grow[0:1, :], in_=g.rearrange("(o k) -> o k", o=1))
+                nc.sync.dma_start(out=gwords[0:1, :].bitcast(BF16), in_=g.rearrange("(o k) -> o k", o=1))
         wr = []
         for c in range(nch):
             m, n0, wd = CHUNKS[c]
@@ -63,13 +64,15 @@ def tile_llamaselfattentionblock_pa_kernel(tc, x, g, wq, wk, out_0, out_1):
         nc.scalar.activation(out=warm[:], in_=neghalf[:], func=ACT.Sin)
         pj = const.tile([P, NT], I32)
         nc.gpsimd.iota(pj[:], pattern=[[0, NT]], base=0, channel_multiplier=1)
-        jj = const.tile([P, NT], I32)
-        nc.gpsimd.iota(jj[:], pattern=[[1, NT]], base=0, channel_multiplier=0)
+        jj = const.tile([P, NT], F32)
+        nc.gpsimd.iota(
+            jj[:], pattern=[[1, NT]], base=0, channel_multiplier=0, allow_small_or_imprecise_dtypes=True
+        )
         pdiff = const.tile([P, 32, B], F32)
         nc.gpsimd.iota(
             pdiff[:], pattern=[[1, 32], [32, B]], base=0, channel_multiplier=-1, allow_small_or_imprecise_dtypes=True
         )
-        perm = const.tile([P, P], BF16)
+        perm = const.tile([P, P], F32)
         nc.gpsimd.tensor_scalar(
             out=perm[:], in0=pdiff[:].rearrange("p l b -> p (l b)"), scalar1=0.0, scalar2=None, op0=ALU.is_equal
         )
@@ -84,20 +87,12 @@ def tile_llamaselfattentionblock_pa_kernel(tc, x, g, wq, wk, out_0, out_1):
             )
         l0i = const.tile([P, NT], I32)
         nc.vector.tensor_scalar(out=l0i[:], in0=pj[:], scalar1=124, scalar2=None, op0=ALU.bitwise_and)
-        lji = const.tile([P, NT], I32)
-        nc.vector.tensor_tensor(out=lji[:], in0=l0i[:], in1=jj[:], op=ALU.bitwise_or)
-        ljt = const.tile([P, NT], F32)
-        nc.vector.tensor_scalar(out=ljt[:], in0=lji[:], scalar1=TURN, scalar2=None, op0=ALU.mult)
-        yy = const.tile([P, NT, 64], F32)
-        for j in range(NT):
-            nc.vector.tensor_scalar(
-                out=yy[:, j, :], in0=th[:], scalar1=ljt[:, j : j + 1], scalar2=0.25, op0=ALU.mult, op1=ALU.add
-            )
-
+        lj = const.tile([P, NT], F32)
+        nc.vector.tensor_tensor(out=lj[:], in0=l0i[:], in1=jj[:], op=ALU.add)
         gp = psum.tile([P, E], BF16, tag="bank", name="gp")
         for hf in range(2):
             sl = slice(512 * hf, 512 * hf + 512)
-            nc.tensor.matmul(out=gp[:, sl], lhsT=ones[:], rhs=grow[:].rearrange("p (i t) -> p t i", t=4)[:, 2 * hf : 2 * hf + 2, :], start=True, stop=True)
+            nc.tensor.matmul(out=gp[:, sl], lhsT=ones[:], rhs=grow[:, sl], start=True, stop=True)
 
         rstds = []
         for j in range(NT):
@@ -130,40 +125,36 @@ def tile_llamaselfattentionblock_pa_kernel(tc, x, g, wq, wk, out_0, out_1):
             nc.gpsimd.tensor_tensor(out=rstd[:], in0=me[:], in1=neghalf[:], op=ALU.pow)
             rstds.append(rstd)
 
-        yi = const.tile([P, NT, 64], I32)
-        nc.vector.tensor_copy(out=yi[:], in_=yy[:])
-        yf = const.tile([P, NT, 64], F32)
-        nc.vector.tensor_copy(out=yf[:], in_=yi[:])
-        rr = const.tile([P, NT, 64], F32)
-        nc.vector.tensor_tensor(out=rr[:], in0=yy[:], in1=yf[:], op=ALU.subtract)
-        nr = const.tile([P, NT, 64], F32)
+        yy = const.tile([P, NT, 64], F32)
         nc.vector.scalar_tensor_tensor(
-            out=nr[:], in0=rr[:], scalar=0.5, in1=rr[:], op0=ALU.is_gt, op1=ALU.subtract
+            out=yy[:],
+            in0=th[:].unsqueeze(1).to_broadcast([P, NT, 64]),
+            scalar=TURN,
+            in1=lj[:].unsqueeze(2).to_broadcast([P, NT, 64]),
+            op0=ALU.mult,
+            op1=ALU.mult,
         )
-        ctab = const.tile([P, NT, 64, 2], F32)
-        nc.scalar.activation(
-            out=ctab[:],
-            in_=nr[:].unsqueeze(3).to_broadcast([P, NT, 64, 2]),
-            func=ACT.Sin,
-            scale=-2.0 * math.pi,
-        )
-
         tps = []
+        nr = const.tile([P, NT, 64], F32)
         for j in range(NT):
             hj = const.tile([P, E], BF16, name="h%d" % j)
             nc.vector.scalar_tensor_tensor(
-                out=hj[:].rearrange("p (t i) -> p t i", t=4),
-                in0=xt[j][:].rearrange("p (i t) -> p t i", t=4),
-                scalar=rstds[j][:, 0:1],
-                in1=gp[:].rearrange("p (t i) -> p t i", t=4),
-                op0=ALU.mult,
-                op1=ALU.mult,
+                out=hj[:], in0=xt[j][:], scalar=rstds[j][:, 0:1], in1=gp[:], op0=ALU.mult, op1=ALU.mult
             )
-            tp = psum.tile([P, 8, P], BF16, tag="bank", name="tp%d" % j)
-            for q in range(8):
-                q0 = 256 * (q % 4) + P * (q // 4)
-                nc.tensor.transpose(out=tp[:, q, :], in_=hj[:, q0 : q0 + P], identity=perm[:])
+            tp = psum.tile([P, NG, 2, P], F32, tag="bank", name="tp%d" % j)
+            hwords = hj[:].bitcast(F32)
+            for gg in range(NG):
+                for u in range(2):
+                    nc.tensor.transpose(
+                        out=tp[:, gg, u, :], in_=hwords[:, 256 * gg + u : 256 * (gg + 1) : 2], identity=perm[:]
+                    )
             tps.append(tp)
+            if j == 0:
+                yi = const.tile([P, NT, 64], I32)
+                nc.vector.tensor_scalar(out=yi[:], in0=yy[:], scalar1=0.25, scalar2=None, op0=ALU.add)
+                nc.vector.scalar_tensor_tensor(
+                    out=nr[:], in0=yy[:], scalar=0.25, in1=yi[:], op0=ALU.add, op1=ALU.subtract
+                )
 
         wgs = [const.tile([P, NG, CHUNKS[c][2], 4], BF16, name="wg%d" % c, align_bytes=64) for c in range(nch)]
 
@@ -200,10 +191,18 @@ def tile_llamaselfattentionblock_pa_kernel(tc, x, g, wq, wk, out_0, out_1):
 
         regroup_g(0, 1, 1.0)
         regroup_s(0, 0)
+        ctab = const.tile([P, NT, 64, 2], F32)
         hgs = []
         for j in range(NT):
-            hg = const.tile([P, NG, P, 4], BF16, name="hg%d" % j, align_bytes=64)
-            nc.scalar.copy(out=hg[:], in_=tps[j][:].rearrange("p (g t) l -> p g l t", t=4))
+            if j == NT - 1:
+                nc.scalar.activation(
+                    out=ctab[:],
+                    in_=nr[:].unsqueeze(3).to_broadcast([P, NT, 64, 2]),
+                    func=ACT.Sin,
+                    scale=2.0 * math.pi,
+                )
+            hg = const.tile([P, NG, P, 2], F32, name="hg%d" % j, align_bytes=64)
+            nc.scalar.copy(out=hg[:], in_=tps[j][:].rearrange("p g u l -> p g l u"))
             hgs.append(hg)
         for c in range(nch):
             for gg in range(NG):
@@ -220,7 +219,7 @@ def tile_llamaselfattentionblock_pa_kernel(tc, x, g, wq, wk, out_0, out_1):
             nc.vector.quantize_mx(
                 out=hw[:, j, :].bitcast(FP8X4),
                 scales=hs[:, j, :],
-                in_=hgs[j][:].rearrange("p g l t -> p (g l t)"),
+                in_=hgs[j][:].rearrange("p g l u -> p (g l u)").bitcast(BF16),
             )
 
         def w_quant(c, gg):
@@ -290,11 +289,9 @@ def tile_llamaselfattentionblock_pa_kernel(tc, x, g, wq, wk, out_0, out_1):
                 )
 
         h_quant(0)
-        regroup_v(0, 0)
         h_quant(1)
         w_quant(0, 0)
         h_quant(2)
-        regroup_v(0, 1)
         h_quant(3)
         regroup_v(1, 0)
         passes_wide(0, 0)

@@ -19,208 +19,135 @@ FLOPS = 2 * B * L * E * 2 * H * HD
 NT = 4
 NG = 2
 TURN = 1.0 / (2.0 * math.pi)
-CHUNKS = [(0, 0, 512), (0, 512, 512), (1, 0, 512), (1, 512, 256), (1, 768, 256)]
-VCOLS = {(1, 0): 256}
-GCOLS = {(0, 1): 256, (2, 0): 256, (3, 0): 256, (4, 0): 256}
-SPLIT_STATS = [True, True, True, False]
+UNITS = [(0, 0), (0, 512), (1, 0), (1, 512)]
+UW = 512
+CHUNKS = [(m, 256 * i, 256) for m in range(2) for i in range(4)]
+LOADS = [0, 1, "g", 2, 3, (0, 0), (0, 1), (1, 0), (1, 1), (2, 0), (2, 1), (3, 0), (3, 1)]
 
 
 def tile_llamaselfattentionblock_pa_kernel(tc, x, g, wq, wk, out_0, out_1):
     nc = tc.nc
-    nch = len(CHUNKS)
     with ExitStack() as ctx:
         const = ctx.enter_context(tc.tile_pool(name="const", bufs=1))
         psum = ctx.enter_context(tc.psum_pool(name="psum", bufs=8))
         ctx.enter_context(tc.manual_schedule())
 
         gwords = const.tile([P, E // 2], I32, name="gwords")
-        nc.gpsimd.memset(gwords[:], 0)
         grow = gwords[:].bitcast(BF16)
+        xt = [const.tile([P, E], BF16, name="x%d" % j) for j in range(NT)]
+        wr = [const.tile([P, NG, 4, UW], BF16, name="wr%d" % u) for u in range(len(UNITS))]
+        wgs = [const.tile([P, NG, ch[2], 4], BF16, name="wg%d" % c, align_bytes=64) for c, ch in enumerate(CHUNKS)]
+        wws = [const.tile([P, NG, ch[2]], U32, name="ww%d" % c, align_bytes=64) for c, ch in enumerate(CHUNKS)]
+        wss = [const.tile([P, NG, ch[2]], U8, name="ws%d" % c, align_bytes=64) for c, ch in enumerate(CHUNKS)]
+        hgs = [const.tile([P, 2, NG, P, 2], F32, name="hg%d" % jp, align_bytes=64) for jp in range(2)]
+        hw = const.tile([P, NT, NG * P], U32, name="hw", align_bytes=64)
+        hs = const.tile([P, NT, NG * P], U8, name="hs", align_bytes=64)
+        ctab = const.tile([P, NT, 64, 2], F32, name="ctab")
+        osb = [const.tile([P, ch[2] // HD, NT, HD], F32, name="osb%d" % c) for c, ch in enumerate(CHUNKS)]
+        msa = [const.tile([P, 1], F32, name="msa%d" % j) for j in range(NT)]
+        msb = [const.tile([P, 1], F32, name="msb%d" % j) for j in range(NT)]
+        rstds = [const.tile([P, 1], F32, name="rstd%d" % j) for j in range(NT)]
+        tps = {}
+        accs = {}
+
         xv = x.rearrange("b l k -> (b l) k").rearrange("(p j) k -> p j k", j=NT)
-        xt = []
-        for j in range(NT):
-            xj = const.tile([P, E], BF16, name="x%d" % j)
-            nc.sync.dma_start(out=xj[:], in_=xv[:, j, :])
-            xt.append(xj)
-            if j == 0:
-                nc.sync.dma_start(out=gwords[0:1, :].bitcast(BF16), in_=g.rearrange("(o k) -> o k", o=1))
-        wr = []
-        for c in range(nch):
-            m, n0, wd = CHUNKS[c]
+
+        def load_x(j):
+            nc.sync.dma_start(out=xt[j][:], in_=xv[:, j, :])
+
+        def load_w(u, gg):
+            m, n0 = UNITS[u]
             w = wq if m == 0 else wk
-            wt = const.tile([P, NG, 4, wd], BF16, name="wr%d" % c)
-            for gg in range(NG):
-                nc.sync.dma_start(
-                    out=wt[:, gg, :, :],
-                    in_=w[512 * gg : 512 * gg + 512, n0 : n0 + wd].rearrange("(p t) n -> p t n", p=P),
-                )
-            wr.append(wt)
-
-        ones = const.tile([P, P], BF16)
-        nc.gpsimd.memset(ones[:], 1.0)
-        neghalf = const.tile([P, 1], F32)
-        nc.gpsimd.memset(neghalf[:], -0.5)
-        warm = const.tile([P, 1], F32)
-        nc.scalar.activation(out=warm[:], in_=neghalf[:], func=ACT.Sin)
-        pj = const.tile([P, NT], I32)
-        nc.gpsimd.iota(pj[:], pattern=[[0, NT]], base=0, channel_multiplier=1)
-        jj = const.tile([P, NT], F32)
-        nc.gpsimd.iota(
-            jj[:], pattern=[[1, NT]], base=0, channel_multiplier=0, allow_small_or_imprecise_dtypes=True
-        )
-        pdiff = const.tile([P, 32, B], F32)
-        nc.gpsimd.iota(
-            pdiff[:], pattern=[[1, 32], [32, B]], base=0, channel_multiplier=-1, allow_small_or_imprecise_dtypes=True
-        )
-        perm = const.tile([P, P], F32)
-        nc.gpsimd.tensor_scalar(
-            out=perm[:], in0=pdiff[:].rearrange("p l b -> p (l b)"), scalar1=0.0, scalar2=None, op0=ALU.is_equal
-        )
-
-        th = const.tile([P, 64], F32)
-        nc.vector.memset(th[:, 0:1], 1.0)
-        ratio = 10000.0 ** (-1.0 / 64.0)
-        for s in range(6):
-            wd = 1 << s
-            nc.vector.tensor_scalar(
-                out=th[:, wd : 2 * wd], in0=th[:, 0:wd], scalar1=ratio**wd, scalar2=None, op0=ALU.mult
+            nc.sync.dma_start(
+                out=wr[u][:, gg, :, :],
+                in_=w[512 * gg : 512 * gg + 512, n0 : n0 + UW].rearrange("(p t) n -> p t n", t=4),
             )
-        l0i = const.tile([P, NT], I32)
-        nc.vector.tensor_scalar(out=l0i[:], in0=pj[:], scalar1=124, scalar2=None, op0=ALU.bitwise_and)
-        lj = const.tile([P, NT], F32)
-        nc.vector.tensor_tensor(out=lj[:], in0=l0i[:], in1=jj[:], op=ALU.add)
-        gp = psum.tile([P, E], BF16, tag="bank", name="gp")
-        for hf in range(2):
-            sl = slice(512 * hf, 512 * hf + 512)
-            nc.tensor.matmul(out=gp[:, sl], lhsT=ones[:], rhs=grow[:, sl], start=True, stop=True)
 
-        rstds = []
-        for j in range(NT):
+        def raw(c, gg, c0, c1):
+            m, n0, wd = CHUNKS[c]
+            u = UNITS.index((m, n0 - n0 % UW))
+            return wr[u][:, gg, :, n0 % UW + c0 : n0 % UW + c1]
+
+        def stats_scalar(j, c1):
+            junk = const.tile([P, c1], BF16, name="junka%d" % j)
+            nc.scalar.activation(
+                out=junk[:], in_=xt[j][:, 0:c1], func=ACT.Square, scale=1.0 / 32.0, accum_out=msa[j][:]
+            )
+
+        def stats_vector(j, c0):
+            junk = const.tile([P, E - c0], F32, name="junkb%d" % j)
+            nc.vector.scalar_tensor_tensor(
+                out=junk[:],
+                in0=xt[j][:, c0:E],
+                scalar=1.0 / 1024.0,
+                in1=xt[j][:, c0:E],
+                op0=ALU.mult,
+                op1=ALU.mult,
+                accum_out=msb[j][:],
+            )
+
+        def make_rstd(j, split):
             me = const.tile([P, 1], F32, name="me%d" % j)
-            msa = const.tile([P, 1], F32, name="msa%d" % j)
-            if SPLIT_STATS[j]:
-                junka = const.tile([P, 512], BF16, name="junka%d" % j)
-                nc.scalar.activation(
-                    out=junka[:], in_=xt[j][:, 0:512], func=ACT.Square, scale=1.0 / 32.0, accum_out=msa[:]
-                )
-                junkb = const.tile([P, 512], F32, name="junkb%d" % j)
-                msb = const.tile([P, 1], F32, name="msb%d" % j)
-                nc.vector.scalar_tensor_tensor(
-                    out=junkb[:],
-                    in0=xt[j][:, 512:1024],
-                    scalar=1.0 / 1024.0,
-                    in1=xt[j][:, 512:1024],
-                    op0=ALU.mult,
-                    op1=ALU.mult,
-                    accum_out=msb[:],
-                )
+            if split:
                 nc.gpsimd.tensor_scalar(
-                    out=me[:], in0=msa[:], scalar1=msb[:, 0:1], scalar2=EPS, op0=ALU.add, op1=ALU.add
+                    out=me[:], in0=msa[j][:], scalar1=msb[j][:, 0:1], scalar2=EPS, op0=ALU.add, op1=ALU.add
                 )
             else:
-                junka = const.tile([P, E], BF16, name="junka%d" % j)
-                nc.scalar.activation(out=junka[:], in_=xt[j][:], func=ACT.Square, scale=1.0 / 32.0, accum_out=msa[:])
-                nc.gpsimd.tensor_scalar(out=me[:], in0=msa[:], scalar1=1.0, scalar2=EPS, op0=ALU.mult, op1=ALU.add)
-            rstd = const.tile([P, 1], F32, name="rstd%d" % j)
-            nc.gpsimd.tensor_tensor(out=rstd[:], in0=me[:], in1=neghalf[:], op=ALU.pow)
-            rstds.append(rstd)
+                nc.gpsimd.tensor_scalar(
+                    out=me[:], in0=msa[j][:], scalar1=1.0, scalar2=EPS, op0=ALU.mult, op1=ALU.add
+                )
+            nc.gpsimd.tensor_tensor(out=rstds[j][:], in0=me[:], in1=neghalf[:], op=ALU.pow)
 
-        yy = const.tile([P, NT, 64], F32)
-        nc.vector.scalar_tensor_tensor(
-            out=yy[:],
-            in0=th[:].unsqueeze(1).to_broadcast([P, NT, 64]),
-            scalar=TURN,
-            in1=lj[:].unsqueeze(2).to_broadcast([P, NT, 64]),
-            op0=ALU.mult,
-            op1=ALU.mult,
-        )
-        tps = []
-        nr = const.tile([P, NT, 64], F32)
-        for j in range(NT):
+        def h_norm(j):
             hj = const.tile([P, E], BF16, name="h%d" % j)
             nc.vector.scalar_tensor_tensor(
                 out=hj[:], in0=xt[j][:], scalar=rstds[j][:, 0:1], in1=gp[:], op0=ALU.mult, op1=ALU.mult
             )
-            tp = psum.tile([P, NG, 2, P], F32, tag="bank", name="tp%d" % j)
+            tps[j] = psum.tile([P, NG, 2, P], F32, tag="bank", name="tp%d" % j)
             hwords = hj[:].bitcast(F32)
             for gg in range(NG):
                 for u in range(2):
                     nc.tensor.transpose(
-                        out=tp[:, gg, u, :], in_=hwords[:, 256 * gg + u : 256 * (gg + 1) : 2], identity=perm[:]
+                        out=tps[j][:, gg, u, :], in_=hwords[:, 256 * gg + u : 256 * (gg + 1) : 2], identity=perm[:]
                     )
-            tps.append(tp)
-            if j == 0:
-                yi = const.tile([P, NT, 64], I32)
-                nc.vector.tensor_scalar(out=yi[:], in0=yy[:], scalar1=0.25, scalar2=None, op0=ALU.add)
-                nc.vector.scalar_tensor_tensor(
-                    out=nr[:], in0=yy[:], scalar=0.25, in1=yi[:], op0=ALU.add, op1=ALU.subtract
-                )
 
-        wgs = [const.tile([P, NG, CHUNKS[c][2], 4], BF16, name="wg%d" % c, align_bytes=64) for c in range(nch)]
+        def h_copy(j):
+            nc.scalar.copy(out=hgs[j // 2][:, j % 2, :, :, :], in_=tps[j][:].rearrange("p g u l -> p g l u"))
+
+        def h_quant(jp):
+            nc.vector.quantize_mx(
+                out=hw[:, 2 * jp : 2 * jp + 2, :].rearrange("p j w -> p (j w)").bitcast(FP8X4),
+                scales=hs[:, 2 * jp : 2 * jp + 2, :].rearrange("p j w -> p (j w)"),
+                in_=hgs[jp][:].rearrange("p j g l u -> p (j g l u)").bitcast(BF16),
+            )
 
         def regroup(eng_copy, c, gg, c0, c1):
             eng_copy(
                 out=wgs[c][:, gg, c0:c1, :].rearrange("p (c i) t -> p c t i", i=4),
-                in_=wr[c][:, gg, :, c0:c1].rearrange("p t (c i) -> p c t i", i=4),
+                in_=raw(c, gg, c0, c1).rearrange("p t (c i) -> p c t i", i=4),
             )
 
-        def regroup_s(c, gg):
-            c1 = CHUNKS[c][2] - GCOLS.get((c, gg), 0)
-            if VCOLS.get((c, gg), 0) < c1:
-                regroup(nc.scalar.copy, c, gg, VCOLS.get((c, gg), 0), c1)
+        def regroup_s(c, gg, c0, c1):
+            regroup(nc.scalar.copy, c, gg, c0, c1)
 
-        def regroup_g(c, gg, one):
-            c1 = CHUNKS[c][2]
-            for c0 in range(c1 - GCOLS[(c, gg)], c1, P):
+        def regroup_v(c, gg, c0, c1):
+            regroup(nc.vector.tensor_copy, c, gg, c0, c1)
+
+        def regroup_g(c, gg, c0, c1, gated):
+            one = 1.0
+            if gated:
+                ot = const.tile([P, 1], F32, name="one%d_%d_%d" % (c, gg, c0))
+                nc.vector.memset(ot[:], 1.0)
+                one = ot[:, 0:1]
+            for a in range(c0, c1, P):
                 nc.gpsimd.tensor_scalar(
-                    out=wgs[c][:, gg, c0 : c0 + P, :],
-                    in0=wr[c][:, gg, :, c0 : c0 + P].rearrange("p t n -> p n t"),
+                    out=wgs[c][:, gg, a : a + P, :],
+                    in0=raw(c, gg, a, a + P).rearrange("p t n -> p n t"),
                     scalar1=one,
                     scalar2=0.0,
                     op0=ALU.mult,
                     op1=ALU.add,
                 )
-
-        def gate(k):
-            one = const.tile([P, 1], F32, name="one%d" % k)
-            nc.vector.memset(one[:], 1.0)
-            return one[:, 0:1]
-
-        def regroup_v(c, gg):
-            regroup(nc.vector.tensor_copy, c, gg, 0, VCOLS[(c, gg)])
-
-        regroup_g(0, 1, 1.0)
-        regroup_s(0, 0)
-        ctab = const.tile([P, NT, 64, 2], F32)
-        hgs = []
-        for j in range(NT):
-            if j == NT - 1:
-                nc.scalar.activation(
-                    out=ctab[:],
-                    in_=nr[:].unsqueeze(3).to_broadcast([P, NT, 64, 2]),
-                    func=ACT.Sin,
-                    scale=2.0 * math.pi,
-                )
-            hg = const.tile([P, NG, P, 2], F32, name="hg%d" % j, align_bytes=64)
-            nc.scalar.copy(out=hg[:], in_=tps[j][:].rearrange("p g u l -> p g l u"))
-            hgs.append(hg)
-        for c in range(nch):
-            for gg in range(NG):
-                if (c, gg) != (0, 0):
-                    regroup_s(c, gg)
-
-        hw = const.tile([P, NT, NG * P], U32, align_bytes=64)
-        hs = const.tile([P, NT, NG * P], U8, align_bytes=64)
-        wws = [const.tile([P, NG, CHUNKS[c][2]], U32, name="ww%d" % c, align_bytes=64) for c in range(nch)]
-        wss = [const.tile([P, NG, CHUNKS[c][2]], U8, name="ws%d" % c, align_bytes=64) for c in range(nch)]
-        accs = {}
-
-        def h_quant(j):
-            nc.vector.quantize_mx(
-                out=hw[:, j, :].bitcast(FP8X4),
-                scales=hs[:, j, :],
-                in_=hgs[j][:].rearrange("p g l u -> p (g l u)").bitcast(BF16),
-            )
 
         def w_quant(c, gg):
             nc.vector.quantize_mx(
@@ -254,66 +181,200 @@ def tile_llamaselfattentionblock_pa_kernel(tc, x, g, wq, wk, out_0, out_1):
                 one_pass(accs[c][j][:], c, j, gg)
 
         def passes_narrow(c):
-            accs[c] = [psum.tile([P, 2, 256], F32, tag="bank", name="acc%d_%d" % (c, jp)) for jp in range(2)]
+            wd = CHUNKS[c][2]
+            nj = 512 // wd
+            accs[c] = [psum.tile([P, nj, wd], F32, tag="bank", name="acc%d_%d" % (c, q)) for q in range(NT // nj)]
             for j in range(NT):
                 for gg in range(NG):
-                    one_pass(accs[c][j // 2][:, j % 2, :], c, j, gg)
+                    one_pass(accs[c][j // nj][:, j % nj, :], c, j, gg)
 
-        def rope_store(c):
+        def rope(c, q):
+            wd = CHUNKS[c][2]
+            nh = wd // HD
+            nj = 512 // wd
+            j0 = nj * q
+            ct = ctab[:].rearrange("p j i e -> p j (i e)")
+            if nj == 1:
+                nc.vector.tensor_tensor(
+                    out=osb[c][:, :, j0, :],
+                    in0=accs[c][q][:].rearrange("p (n d) -> p n d", d=HD),
+                    in1=ct[:, j0, :].unsqueeze(1).to_broadcast([P, nh, HD]),
+                    op=ALU.mult,
+                )
+            elif nh == 1:
+                nc.vector.tensor_tensor(
+                    out=osb[c][:, 0, j0 : j0 + nj, :], in0=accs[c][q][:], in1=ct[:, j0 : j0 + nj, :], op=ALU.mult
+                )
+            else:
+                nc.vector.tensor_tensor(
+                    out=osb[c][:, :, j0 : j0 + nj, :],
+                    in0=accs[c][q][:].rearrange("p j (n d) -> p n j d", d=HD),
+                    in1=ct[:, j0 : j0 + nj, :].unsqueeze(1).to_broadcast([P, nh, nj, HD]),
+                    op=ALU.mult,
+                )
+
+        def store(c):
             m, n0, wd = CHUNKS[c]
             om = out_0 if m == 0 else out_1
             nh = wd // HD
             h0 = n0 // HD
-            osb = const.tile([P, nh, NT, HD], F32, name="osb%d" % c)
-            ct = ctab[:].rearrange("p j i e -> p j (i e)")
-            if wd == 512:
-                for j in range(NT):
-                    nc.vector.tensor_tensor(
-                        out=osb[:, :, j, :],
-                        in0=accs[c][j][:].rearrange("p (n d) -> p n d", d=HD),
-                        in1=ct[:, j, :].unsqueeze(1).to_broadcast([P, nh, HD]),
-                        op=ALU.mult,
-                    )
-            else:
-                for jp in range(2):
-                    nc.vector.tensor_tensor(
-                        out=osb[:, :, 2 * jp : 2 * jp + 2, :],
-                        in0=accs[c][jp][:].rearrange("p j (n d) -> p n j d", d=HD),
-                        in1=ct[:, 2 * jp : 2 * jp + 2, :].unsqueeze(1).to_broadcast([P, nh, 2, HD]),
-                        op=ALU.mult,
-                    )
             for b in range(B):
                 nc.sync.dma_start(
                     out=om[b, h0 : h0 + nh, :, :].rearrange("n (lh j) d -> lh n (j d)", j=NT),
-                    in_=osb[b:P:4, :, :, :].rearrange("p n j d -> p n (j d)"),
+                    in_=osb[c][b:P:4, :, :, :].rearrange("p n j d -> p n (j d)"),
                 )
 
+        def rope_store(c):
+            for q in range(len(accs[c])):
+                rope(c, q)
+            store(c)
+
+        nc.gpsimd.memset(gwords[:], 0)
+        ones = const.tile([P, P], BF16)
+        nc.gpsimd.memset(ones[:], 1.0)
+        neghalf = const.tile([P, 1], F32)
+        nc.gpsimd.memset(neghalf[:], -0.5)
+        warm = const.tile([P, 1], F32)
+        nc.scalar.activation(out=warm[:], in_=neghalf[:], func=ACT.Sin)
+        pj = const.tile([P, NT], I32)
+        nc.gpsimd.iota(pj[:], pattern=[[0, NT]], base=0, channel_multiplier=1)
+        jj = const.tile([P, NT], F32)
+        nc.gpsimd.iota(
+            jj[:], pattern=[[1, NT]], base=0, channel_multiplier=0, allow_small_or_imprecise_dtypes=True
+        )
+        pdiff = const.tile([P, 32, B], F32)
+        nc.gpsimd.iota(
+            pdiff[:], pattern=[[1, 32], [32, B]], base=0, channel_multiplier=-1, allow_small_or_imprecise_dtypes=True
+        )
+        perm = const.tile([P, P], F32)
+        nc.gpsimd.tensor_scalar(
+            out=perm[:], in0=pdiff[:].rearrange("p l b -> p (l b)"), scalar1=0.0, scalar2=None, op0=ALU.is_equal
+        )
+
+        for step in LOADS:
+            if step == "g":
+                nc.sync.dma_start(out=gwords[0:1, :].bitcast(BF16), in_=g.rearrange("(o k) -> o k", o=1))
+            elif isinstance(step, int):
+                load_x(step)
+            else:
+                load_w(step[0], step[1])
+
+        th = const.tile([P, 64], F32)
+        nc.vector.memset(th[:, 0:1], 1.0)
+        ratio = 10000.0 ** (-1.0 / 64.0)
+        for s in range(6):
+            wd = 1 << s
+            nc.vector.tensor_scalar(
+                out=th[:, wd : 2 * wd], in0=th[:, 0:wd], scalar1=ratio**wd, scalar2=None, op0=ALU.mult
+            )
+        l0i = const.tile([P, NT], I32)
+        nc.vector.tensor_scalar(out=l0i[:], in0=pj[:], scalar1=124, scalar2=None, op0=ALU.bitwise_and)
+        lj = const.tile([P, NT], F32)
+        nc.vector.tensor_tensor(out=lj[:], in0=l0i[:], in1=jj[:], op=ALU.add)
+        yy = const.tile([P, NT, 64], F32)
+        yi = const.tile([P, NT, 64], I32)
+        nr = const.tile([P, NT, 64], F32)
+
+        def table_product():
+            nc.vector.scalar_tensor_tensor(
+                out=yy[:],
+                in0=th[:].unsqueeze(1).to_broadcast([P, NT, 64]),
+                scalar=TURN,
+                in1=lj[:].unsqueeze(2).to_broadcast([P, NT, 64]),
+                op0=ALU.mult,
+                op1=ALU.mult,
+            )
+
+        def table_int():
+            nc.vector.tensor_scalar(out=yi[:], in0=yy[:], scalar1=0.25, scalar2=None, op0=ALU.add)
+
+        def table_rest():
+            nc.vector.scalar_tensor_tensor(
+                out=nr[:], in0=yy[:], scalar=0.25, in1=yi[:], op0=ALU.add, op1=ALU.subtract
+            )
+
+        def table_sine():
+            nc.scalar.activation(
+                out=ctab[:],
+                in_=nr[:].unsqueeze(3).to_broadcast([P, NT, 64, 2]),
+                func=ACT.Sin,
+                scale=2.0 * math.pi,
+            )
+
+        gp = psum.tile([P, E], BF16, tag="bank", name="gp")
+        for hf in range(2):
+            sl = slice(512 * hf, 512 * hf + 512)
+            nc.tensor.matmul(out=gp[:, sl], lhsT=ones[:], rhs=grow[:, sl], start=True, stop=True)
+
+        table_product()
+        stats_scalar(0, 512)
+        stats_vector(0, 512)
+        make_rstd(0, True)
+        table_int()
+        stats_scalar(1, 512)
+        stats_vector(1, 512)
+        make_rstd(1, True)
+        stats_scalar(2, 1024)
+        stats_scalar(3, 1024)
+        make_rstd(2, False)
+        make_rstd(3, False)
+        regroup_g(0, 1, 128, 256, False)
+        regroup_g(1, 0, 128, 256, False)
+        h_norm(0)
+        table_rest()
+        h_norm(1)
+        h_norm(2)
+        h_norm(3)
+        regroup_s(0, 0, 0, 256)
+        h_copy(0)
+        regroup_s(0, 1, 0, 128)
+        h_copy(1)
+        h_copy(2)
+        table_sine()
+        h_copy(3)
+        regroup_s(1, 0, 0, 128)
+        regroup_s(2, 0, 0, 128)
+        regroup_s(2, 1, 0, 256)
+        regroup_s(3, 0, 0, 128)
+        regroup_s(3, 1, 0, 256)
+        regroup_s(4, 0, 0, 128)
+        regroup_s(4, 1, 0, 256)
+        regroup_s(5, 0, 0, 128)
+        regroup_s(5, 1, 0, 256)
+        regroup_s(6, 0, 0, 128)
+        regroup_s(6, 1, 0, 256)
+        regroup_s(7, 0, 0, 128)
+        regroup_s(7, 1, 0, 256)
         h_quant(0)
+        w_quant_both(0)
+        regroup_v(1, 1, 0, 256)
         h_quant(1)
-        w_quant(0, 0)
-        h_quant(2)
-        h_quant(3)
-        regroup_v(1, 0)
-        passes_wide(0, 0)
-        w_quant(0, 1)
-        passes_wide(0, 1)
-        w_quant(1, 0)
-        passes_wide(1, 0)
-        regroup_g(2, 0, gate(0))
+        passes_narrow(0)
+        w_quant_both(1)
+        passes_narrow(1)
+        regroup_g(2, 0, 128, 256, True)
         rope_store(0)
-        w_quant(1, 1)
-        passes_wide(1, 1)
-        w_quant(2, 0)
-        passes_wide(2, 0)
-        regroup_g(3, 0, gate(1))
+        w_quant_both(2)
+        passes_narrow(2)
+        regroup_g(3, 0, 128, 256, True)
         rope_store(1)
-        w_quant(2, 1)
-        passes_wide(2, 1)
         w_quant_both(3)
         passes_narrow(3)
-        regroup_g(4, 0, gate(2))
+        regroup_g(4, 0, 128, 256, True)
         rope_store(2)
         w_quant_both(4)
         passes_narrow(4)
+        regroup_g(5, 0, 128, 256, True)
         rope_store(3)
+        w_quant_both(5)
+        passes_narrow(5)
+        regroup_g(6, 0, 128, 256, True)
         rope_store(4)
+        w_quant_both(6)
+        passes_narrow(6)
+        regroup_g(7, 0, 128, 256, True)
+        rope_store(5)
+        w_quant_both(7)
+        passes_narrow(7)
+        rope_store(6)
+        rope_store(7)

@@ -89,7 +89,7 @@ def tile_llamaselfattentionblock_pa_kernel(tc, x, g, wq, wk, out_0, out_1):
         def make_rstd(j, split):
             me = const.tile([P, 1], F32, name="me%d" % j)
             if split:
-                nc.gpsimd.tensor_scalar(
+                nc.vector.tensor_scalar(
                     out=me[:], in0=msa[j][:], scalar1=msb[j][:, 0:1], scalar2=EPS, op0=ALU.add, op1=ALU.add
                 )
             else:
@@ -229,13 +229,12 @@ def tile_llamaselfattentionblock_pa_kernel(tc, x, g, wq, wk, out_0, out_1):
                 rope(c, q)
             store(c)
 
-        nc.gpsimd.memset(gwords[:], 0)
-        ones = const.tile([P, P], BF16)
-        nc.gpsimd.memset(ones[:], 1.0)
         neghalf = const.tile([P, 1], F32)
-        nc.gpsimd.memset(neghalf[:], -0.5)
+        nc.vector.memset(neghalf[:], -0.5)
+        nc.vector.memset(gwords[:], 0)
         warm = const.tile([P, 1], F32)
         nc.scalar.activation(out=warm[:], in_=neghalf[:], func=ACT.Sin)
+        ones = const.tile([P, P], BF16)
         pj = const.tile([P, NT], I32)
         nc.gpsimd.iota(pj[:], pattern=[[0, NT]], base=0, channel_multiplier=1)
         jj = const.tile([P, NT], F32)
@@ -247,18 +246,14 @@ def tile_llamaselfattentionblock_pa_kernel(tc, x, g, wq, wk, out_0, out_1):
             pdiff[:], pattern=[[1, 32], [32, B]], base=0, channel_multiplier=-1, allow_small_or_imprecise_dtypes=True
         )
         perm = const.tile([P, P], F32)
-        nc.gpsimd.tensor_scalar(
-            out=perm[:], in0=pdiff[:].rearrange("p l b -> p (l b)"), scalar1=0.0, scalar2=None, op0=ALU.is_equal
-        )
 
-        for step in LOADS:
-            if step == "g":
-                nc.sync.dma_start(out=gwords[0:1, :].bitcast(BF16), in_=g.rearrange("(o k) -> o k", o=1))
-            elif isinstance(step, int):
-                load_x(step)
-            else:
-                load_w(step[0], step[1])
+        def make_perm():
+            nc.vector.tensor_scalar(
+                out=perm[:], in0=pdiff[:].rearrange("p l b -> p (l b)"), scalar1=0.0, scalar2=None, op0=ALU.is_equal
+            )
 
+        l0i = const.tile([P, NT], I32)
+        lj = const.tile([P, NT], F32)
         th = const.tile([P, 64], F32)
         nc.vector.memset(th[:, 0:1], 1.0)
         ratio = 10000.0 ** (-1.0 / 64.0)
@@ -267,10 +262,22 @@ def tile_llamaselfattentionblock_pa_kernel(tc, x, g, wq, wk, out_0, out_1):
             nc.vector.tensor_scalar(
                 out=th[:, wd : 2 * wd], in0=th[:, 0:wd], scalar1=ratio**wd, scalar2=None, op0=ALU.mult
             )
-        l0i = const.tile([P, NT], I32)
-        nc.vector.tensor_scalar(out=l0i[:], in0=pj[:], scalar1=124, scalar2=None, op0=ALU.bitwise_and)
-        lj = const.tile([P, NT], F32)
-        nc.vector.tensor_tensor(out=lj[:], in0=l0i[:], in1=jj[:], op=ALU.add)
+            if s == 1:
+                nc.vector.tensor_scalar(out=l0i[:], in0=pj[:], scalar1=124, scalar2=None, op0=ALU.bitwise_and)
+            elif s == 2:
+                nc.vector.memset(ones[:], 1.0)
+            elif s == 3:
+                nc.vector.tensor_tensor(out=lj[:], in0=l0i[:], in1=jj[:], op=ALU.add)
+            elif s == 4:
+                make_perm()
+        for step in LOADS:
+            if step == "g":
+                nc.sync.dma_start(out=gwords[0:1, :].bitcast(BF16), in_=g.rearrange("(o k) -> o k", o=1))
+            elif isinstance(step, int):
+                load_x(step)
+            else:
+                load_w(step[0], step[1])
+
         yy = const.tile([P, NT, 64], F32)
         yi = const.tile([P, NT, 64], I32)
         nr = const.tile([P, NT, 64], F32)
@@ -306,13 +313,13 @@ def tile_llamaselfattentionblock_pa_kernel(tc, x, g, wq, wk, out_0, out_1):
             sl = slice(512 * hf, 512 * hf + 512)
             nc.tensor.matmul(out=gp[:, sl], lhsT=ones[:], rhs=grow[:, sl], start=True, stop=True)
 
-        table_product()
         stats_scalar(0, 512)
         stats_vector(0, 512)
+        table_product()
         make_rstd(0, True)
-        table_int()
         stats_scalar(1, 512)
         stats_vector(1, 512)
+        table_int()
         make_rstd(1, True)
         stats_scalar(2, 1024)
         stats_scalar(3, 1024)

@@ -133,21 +133,20 @@ def tile_llamaselfattentionblock_pa_kernel(tc, x, g, wq, wk, out_0, out_1):
         def regroup_v(c, gg, c0, c1):
             regroup(nc.vector.tensor_copy, c, gg, c0, c1)
 
-        def regroup_g(c, gg, c0, c1, gated):
-            one = 1.0
-            if gated:
-                ot = const.tile([P, 1], F32, name="one%d_%d_%d" % (c, gg, c0))
-                nc.vector.memset(ot[:], 1.0)
-                one = ot[:, 0:1]
-            for a in range(c0, c1, P):
-                nc.gpsimd.tensor_scalar(
-                    out=wgs[c][:, gg, a : a + P, :],
-                    in0=raw(c, gg, a, a + P).rearrange("p t n -> p n t"),
-                    scalar1=one,
-                    scalar2=0.0,
-                    op0=ALU.mult,
-                    op1=ALU.add,
-                )
+        def gate(c):
+            ot = const.tile([P, 1], F32, name="one%d" % c)
+            nc.vector.memset(ot[:], 1.0)
+            return ot[:, 0:1]
+
+        def regroup_g(c, gg, c0, c1, one):
+            nc.gpsimd.tensor_scalar(
+                out=wgs[c][:, gg, c0:c1, :],
+                in0=raw(c, gg, c0, c1).rearrange("p t n -> p n t"),
+                scalar1=one,
+                scalar2=0.0,
+                op0=ALU.mult,
+                op1=ALU.add,
+            )
 
         def w_quant(c, gg):
             nc.vector.quantize_mx(
@@ -325,10 +324,10 @@ def tile_llamaselfattentionblock_pa_kernel(tc, x, g, wq, wk, out_0, out_1):
         stats_scalar(3, 1024)
         make_rstd(2, False)
         make_rstd(3, False)
-        regroup_g(0, 1, 128, 256, False)
-        regroup_g(1, 0, 128, 256, False)
-        h_norm(0)
+        regroup_g(0, 1, 128, 256, 1.0)
+        regroup_g(1, 0, 128, 256, 1.0)
         table_rest()
+        h_norm(0)
         h_norm(1)
         h_norm(2)
         h_norm(3)
@@ -340,46 +339,52 @@ def tile_llamaselfattentionblock_pa_kernel(tc, x, g, wq, wk, out_0, out_1):
         table_sine()
         h_copy(3)
         regroup_s(1, 0, 0, 128)
-        regroup_s(2, 0, 0, 128)
+        regroup_s(2, 0, 0, 96)
         regroup_s(2, 1, 0, 256)
-        regroup_s(3, 0, 0, 128)
+        regroup_s(3, 0, 0, 96)
         regroup_s(3, 1, 0, 256)
-        regroup_s(4, 0, 0, 128)
+        regroup_s(4, 0, 0, 96)
         regroup_s(4, 1, 0, 256)
-        regroup_s(5, 0, 0, 128)
+        regroup_s(5, 0, 0, 96)
         regroup_s(5, 1, 0, 256)
-        regroup_s(6, 0, 0, 128)
+        regroup_s(6, 0, 0, 96)
         regroup_s(6, 1, 0, 256)
-        regroup_s(7, 0, 0, 128)
+        regroup_s(7, 0, 0, 96)
         regroup_s(7, 1, 0, 256)
         h_quant(0)
         w_quant_both(0)
         regroup_v(1, 1, 0, 256)
         h_quant(1)
         passes_narrow(0)
+        one = gate(2)
         w_quant_both(1)
         passes_narrow(1)
-        regroup_g(2, 0, 128, 256, True)
+        regroup_g(2, 0, 96, 256, one)
         rope_store(0)
+        one = gate(3)
         w_quant_both(2)
         passes_narrow(2)
-        regroup_g(3, 0, 128, 256, True)
+        regroup_g(3, 0, 96, 256, one)
         rope_store(1)
+        one = gate(4)
         w_quant_both(3)
         passes_narrow(3)
-        regroup_g(4, 0, 128, 256, True)
+        regroup_g(4, 0, 96, 256, one)
         rope_store(2)
+        one = gate(5)
         w_quant_both(4)
         passes_narrow(4)
-        regroup_g(5, 0, 128, 256, True)
+        regroup_g(5, 0, 96, 256, one)
         rope_store(3)
+        one = gate(6)
         w_quant_both(5)
         passes_narrow(5)
-        regroup_g(6, 0, 128, 256, True)
+        regroup_g(6, 0, 96, 256, one)
         rope_store(4)
+        one = gate(7)
         w_quant_both(6)
         passes_narrow(6)
-        regroup_g(7, 0, 128, 256, True)
+        regroup_g(7, 0, 96, 256, one)
         rope_store(5)
         w_quant_both(7)
         passes_narrow(7)

import math
from contextlib import ExitStack

import concourse.mybir as mybir

FP8X4 = mybir.dt.float8_e4m3fn_x4
BF16 = mybir.dt.bfloat16
F32 = mybir.dt.float32
I32 = mybir.dt.int32
U32 = mybir.dt.uint32
U8 = mybir.dt.uint8
ALU = mybir.AluOpType
ACT = mybir.ActivationFunctionType

P = 128
B, L, E, H, HD = 4, 128, 1024, 8, 128
EPS = 1e-6
FLOPS = 2 * B * L * E * 2 * H * HD
NT = 4
NG = 2
TURN = 1.0 / (2.0 * math.pi)
UNITS = [(0, 0), (0, 512), (1, 0), (1, 512)]
UW = 512
CHUNKS = [(m, 256 * i, 256) for m in range(2) for i in range(4)]
LOADS = [0, 1, "g", 2, 3, (0, 0), (0, 1), (1, 0), (1, 1), (2, 0), (2, 1), (3, 0), (3, 1)]


def tile_llamaselfattentionblock_pa_kernel(tc, x, g, wq, wk, out_0, out_1):
    nc = tc.nc
    with ExitStack() as ctx:
        const = ctx.enter_context(tc.tile_pool(name="const", bufs=1))
        psum = ctx.enter_context(tc.psum_pool(name="psum", bufs=8))
        ctx.enter_context(tc.manual_schedule())

        gwords = const.tile([P, E // 2], I32, name="gwords")
        grow = gwords[:].bitcast(BF16)
        xt = [const.tile([P, E], BF16, name="x%d" % j) for j in range(NT)]
        wr = [const.tile([P, NG, 4, UW], BF16, name="wr%d" % u) for u in range(len(UNITS))]
        wgs = [const.tile([P, NG, ch[2], 4], BF16, name="wg%d" % c, align_bytes=64) for c, ch in enumerate(CHUNKS)]
        wws = [const.tile([P, NG, ch[2]], U32, name="ww%d" % c, align_bytes=64) for c, ch in enumerate(CHUNKS)]
        wss = [const.tile([P, NG, ch[2]], U8, name="ws%d" % c, align_bytes=64) for c, ch in enumerate(CHUNKS)]
        hgs = [const.tile([P, 2, NG, P, 2], F32, name="hg%d" % jp, align_bytes=64) for jp in range(2)]
        hw = const.tile([P, NT, NG * P], U32, name="hw", align_bytes=64)
        hs = const.tile([P, NT, NG * P], U8, name="hs", align_bytes=64)
        ctab = const.tile([P, NT, 64, 2], F32, name="ctab")
        osb = [const.tile([P, ch[2] // HD, NT, HD], F32, name="osb%d" % c) for c, ch in enumerate(CHUNKS)]
        msa = [const.tile([P, 1], F32, name="msa%d" % j) for j in range(NT)]
        msb = [const.tile([P, 1], F32, name="msb%d" % j) for j in range(NT)]
        rstds = [const.tile([P, 1], F32, name="rstd%d" % j) for j in range(NT)]
        tps = {}
        accs = {}

        xv = x.rearrange("b l k -> (b l) k").rearrange("(p j) k -> p j k", j=NT)

        def load_x(j):
            nc.sync.dma_start(out=xt[j][:], in_=xv[:, j, :])

        def load_w(u, gg):
            m, n0 = UNITS[u]
            w = wq if m == 0 else wk
            nc.sync.dma_start(
                out=wr[u][:, gg, :, :],
                in_=w[512 * gg : 512 * gg + 512, n0 : n0 + UW].rearrange("(p t) n -> p t n", t=4),
            )

        def raw(c, gg, c0, c1):
            m, n0, wd = CHUNKS[c]
            u = UNITS.index((m, n0 - n0 % UW))
            return wr[u][:, gg, :, n0 % UW + c0 : n0 % UW + c1]

        def stats_scalar(j, c1):
            junk = const.tile([P, c1], BF16, name="junka%d" % j)
            nc.scalar.activation(
                out=junk[:], in_=xt[j][:, 0:c1], func=ACT.Square, scale=1.0 / 32.0, accum_out=msa[j][:]
            )

        def stats_vector(j, c0):
            junk = const.tile([P, E - c0], F32, name="junkb%d" % j)
            nc.vector.scalar_tensor_tensor(
                out=junk[:],
                in0=xt[j][:, c0:E],
                scalar=1.0 / 1024.0,
                in1=xt[j][:, c0:E],
                op0=ALU.mult,
                op1=ALU.mult,
                accum_out=msb[j][:],
            )

        def make_rstd(j, split):
            me = const.tile([P, 1], F32, name="me%d" % j)
            if split:
                nc.vector.tensor_scalar(
                    out=me[:], in0=msa[j][:], scalar1=msb[j][:, 0:1], scalar2=EPS, op0=ALU.add, op1=ALU.add
                )
            else:
                nc.gpsimd.tensor_scalar(
                    out=me[:], in0=msa[j][:], scalar1=1.0, scalar2=EPS, op0=ALU.mult, op1=ALU.add
                )
            nc.gpsimd.tensor_tensor(out=rstds[j][:], in0=me[:], in1=neghalf[:], op=ALU.pow)

        def h_norm(j):
            hj = const.tile([P, E], BF16, name="h%d" % j)
            nc.vector.scalar_tensor_tensor(
                out=hj[:], in0=xt[j][:], scalar=rstds[j][:, 0:1], in1=gp[:], op0=ALU.mult, op1=ALU.mult
            )
            tps[j] = psum.tile([P, NG, 2, P], F32, tag="bank", name="tp%d" % j)
            hwords = hj[:].bitcast(F32)
            for gg in range(NG):
                for u in range(2):
                    nc.tensor.transpose(
                        out=tps[j][:, gg, u, :], in_=hwords[:, 256 * gg + u : 256 * (gg + 1) : 2], identity=perm[:]
                    )

        def h_copy(j):
            nc.scalar.copy(out=hgs[j // 2][:, j % 2, :, :, :], in_=tps[j][:].rearrange("p g u l -> p g l u"))

        def h_quant(jp):
            nc.vector.quantize_mx(
                out=hw[:, 2 * jp : 2 * jp + 2, :].rearrange("p j w -> p (j w)").bitcast(FP8X4),
                scales=hs[:, 2 * jp : 2 * jp + 2, :].rearrange("p j w -> p (j w)"),
                in_=hgs[jp][:].rearrange("p j g l u -> p (j g l u)").bitcast(BF16),
            )

        def regroup(eng_copy, c, gg, c0, c1):
            eng_copy(
                out=wgs[c][:, gg, c0:c1, :].rearrange("p (c i) t -> p c t i", i=4),
                in_=raw(c, gg, c0, c1).rearrange("p t (c i) -> p c t i", i=4),
            )

        def regroup_s(c, gg, c0, c1):
            regroup(nc.scalar.copy, c, gg, c0, c1)

        def regroup_v(c, gg, c0, c1):
            regroup(nc.vector.tensor_copy, c, gg, c0, c1)

        def gate(c):
            ot = const.tile([P, 1], F32, name="one%d" % c)
            nc.vector.memset(ot[:], 1.0)
            return ot[:, 0:1]

        def regroup_g(c, gg, c0, c1, one):
            nc.gpsimd.tensor_scalar(
                out=wgs[c][:, gg, c0:c1, :],
                in0=raw(c, gg, c0, c1).rearrange("p t n -> p n t"),
                scalar1=one,
                scalar2=0.0,
                op0=ALU.mult,
                op1=ALU.add,
            )

        def w_quant(c, gg):
            nc.vector.quantize_mx(
                out=wws[c][:, gg, :].bitcast(FP8X4),
                scales=wss[c][:, gg, :],
                in_=wgs[c][:, gg, :, :].rearrange("p n t -> p (n t)"),
            )

        def w_quant_both(c):
            nc.vector.quantize_mx(
                out=wws[c][:].rearrange("p g n -> p (g n)").bitcast(FP8X4),
                scales=wss[c][:].rearrange("p g n -> p (g n)"),
                in_=wgs[c][:].rearrange("p g n t -> p (g n t)"),
            )

        def one_pass(acc, c, j, gg):
            nc.tensor.matmul_mx(
                out=acc,
                lhsT=hw[:, j, P * gg : P * gg + P].bitcast(FP8X4),
                lhsT_scale=hs[:, j, P * gg : P * gg + P],
                rhs=wws[c][:, gg, :].bitcast(FP8X4),
                rhs_scale=wss[c][:, gg, :],
                start=(gg == 0),
                stop=(gg == NG - 1),
            )

        def passes_wide(c, gg):
            if gg == 0:
                accs[c] = [psum.tile([P, 512], F32, tag="bank", name="acc%d_%d" % (c, j)) for j in range(NT)]
            for j in range(NT):
                one_pass(accs[c][j][:], c, j, gg)

        def passes_narrow(c):
            wd = CHUNKS[c][2]
            nj = 512 // wd
            accs[c] = [psum.tile([P, nj, wd], F32, tag="bank", name="acc%d_%d" % (c, q)) for q in range(NT // nj)]
            for j in range(NT):
                for gg in range(NG):
                    one_pass(accs[c][j // nj][:, j % nj, :], c, j, gg)

        def rope(c, q):
            wd = CHUNKS[c][2]
            nh = wd // HD
            nj = 512 // wd
            j0 = nj * q
            ct = ctab[:].rearrange("p j i e -> p j (i e)")
            if nj == 1:
                nc.vector.tensor_tensor(
                    out=osb[c][:, :, j0, :],
                    in0=accs[c][q][:].rearrange("p (n d) -> p n d", d=HD),
                    in1=ct[:, j0, :].unsqueeze(1).to_broadcast([P, nh, HD]),
                    op=ALU.mult,
                )
            elif nh == 1:
                nc.vector.tensor_tensor(
                    out=osb[c][:, 0, j0 : j0 + nj, :], in0=accs[c][q][:], in1=ct[:, j0 : j0 + nj, :], op=ALU.mult
                )
            else:
                nc.vector.tensor_tensor(
                    out=osb[c][:, :, j0 : j0 + nj, :],
                    in0=accs[c][q][:].rearrange("p j (n d) -> p n j d", d=HD),
                    in1=ct[:, j0 : j0 + nj, :].unsqueeze(1).to_broadcast([P, nh, nj, HD]),
                    op=ALU.mult,
                )

        def store(c):
            m, n0, wd = CHUNKS[c]
            om = out_0 if m == 0 else out_1
            nh = wd // HD
            h0 = n0 // HD
            for b in range(B):
                nc.sync.dma_start(
                    out=om[b, h0 : h0 + nh, :, :].rearrange("n (lh j) d -> lh n (j d)", j=NT),
                    in_=osb[c][b:P:4, :, :, :].rearrange("p n j d -> p n (j d)"),
                )

        def rope_store(c):
            for q in range(len(accs[c])):
                rope(c, q)
            store(c)

        neghalf = const.tile([P, 1], F32)
        nc.vector.memset(neghalf[:], -0.5)
        nc.vector.memset(gwords[:], 0)
        warm = const.tile([P, 1], F32)
        nc.scalar.activation(out=warm[:], in_=neghalf[:], func=ACT.Sin)
        ones = const.tile([P, P], BF16)
        pj = const.tile([P, NT], I32)
        nc.gpsimd.iota(pj[:], pattern=[[0, NT]], base=0, channel_multiplier=1)
        jj = const.tile([P, NT], F32)
        nc.gpsimd.iota(
            jj[:], pattern=[[1, NT]], base=0, channel_multiplier=0, allow_small_or_imprecise_dtypes=True
        )
        pdiff = const.tile([P, 32, B], F32)
        nc.gpsimd.iota(
            pdiff[:], pattern=[[1, 32], [32, B]], base=0, channel_multiplier=-1, allow_small_or_imprecise_dtypes=True
        )
        perm = const.tile([P, P], F32)

        def make_perm():
            nc.vector.tensor_scalar(
                out=perm[:], in0=pdiff[:].rearrange("p l b -> p (l b)"), scalar1=0.0, scalar2=None, op0=ALU.is_equal
            )

        l0i = const.tile([P, NT], I32)
        lj = const.tile([P, NT], F32)
        th = const.tile([P, 64], F32)
        nc.vector.memset(th[:, 0:1], 1.0)
        ratio = 10000.0 ** (-1.0 / 64.0)
        for s in range(6):
            wd = 1 << s
            nc.vector.tensor_scalar(
                out=th[:, wd : 2 * wd], in0=th[:, 0:wd], scalar1=ratio**wd, scalar2=None, op0=ALU.mult
            )
            if s == 1:
                nc.vector.tensor_scalar(out=l0i[:], in0=pj[:], scalar1=124, scalar2=None, op0=ALU.bitwise_and)
            elif s == 2:
                nc.vector.memset(ones[:], 1.0)
            elif s == 3:
                nc.vector.tensor_tensor(out=lj[:], in0=l0i[:], in1=jj[:], op=ALU.add)
            elif s == 4:
                make_perm()
        for step in LOADS:
            if step == "g":
                nc.sync.dma_start(out=gwords[0:1, :].bitcast(BF16), in_=g.rearrange("(o k) -> o k", o=1))
            elif isinstance(step, int):
                load_x(step)
            else:
                load_w(step[0], step[1])

        yy = const.tile([P, NT, 64], F32)
        yi = const.tile([P, NT, 64], I32)
        nr = const.tile([P, NT, 64], F32)

        def table_product():
            nc.vector.scalar_tensor_tensor(
                out=yy[:],
                in0=th[:].unsqueeze(1).to_broadcast([P, NT, 64]),
                scalar=TURN,
                in1=lj[:].unsqueeze(2).to_broadcast([P, NT, 64]),
                op0=ALU.mult,
                op1=ALU.mult,
            )

        def table_int():
            nc.vector.tensor_scalar(out=yi[:], in0=yy[:], scalar1=0.25, scalar2=None, op0=ALU.add)

        def table_rest():
            nc.vector.scalar_tensor_tensor(
                out=nr[:], in0=yy[:], scalar=0.25, in1=yi[:], op0=ALU.add, op1=ALU.subtract
            )

        def table_sine():
            nc.scalar.activation(
                out=ctab[:],
                in_=nr[:].unsqueeze(3).to_broadcast([P, NT, 64, 2]),
                func=ACT.Sin,
                scale=2.0 * math.pi,
            )

        gp = psum.tile([P, E], BF16, tag="bank", name="gp")
        for hf in range(2):
            sl = slice(512 * hf, 512 * hf + 512)
            nc.tensor.matmul(out=gp[:, sl], lhsT=ones[:], rhs=grow[:, sl], start=True, stop=True)

        stats_scalar(0, 512)
        stats_vector(0, 512)
        table_product()
        make_rstd(0, True)
        stats_scalar(1, 512)
        stats_vector(1, 512)
        table_int()
        make_rstd(1, True)
        stats_scalar(2, 1024)
        stats_scalar(3, 1024)
        make_rstd(2, False)
        make_rstd(3, False)
        regroup_g(0, 1, 128, 256, 1.0)
        regroup_g(1, 0, 128, 256, 1.0)
        table_rest()
        h_norm(0)
        h_norm(1)
        h_norm(2)
        h_norm(3)
        regroup_s(0, 0, 0, 256)
        h_copy(0)
        regroup_s(0, 1, 0, 128)
        h_copy(1)
        h_copy(2)
        table_sine()
        h_copy(3)
        regroup_s(1, 0, 0, 128)
        regroup_s(2, 0, 0, 96)
        regroup_s(2, 1, 0, 256)
        regroup_s(3, 0, 0, 96)
        regroup_s(3, 1, 0, 256)
        regroup_s(4, 0, 0, 96)
        regroup_s(4, 1, 0, 256)
        regroup_s(5, 0, 0, 96)
        regroup_s(5, 1, 0, 256)
        regroup_s(6, 0, 0, 96)
        regroup_s(6, 1, 0, 256)
        regroup_s(7, 0, 0, 96)
        regroup_s(7, 1, 0, 256)
        h_quant(0)
        w_quant_both(0)
        regroup_v(1, 1, 0, 256)
        h_quant(1)
        passes_narrow(0)
        one = gate(2)
        w_quant_both(1)
        passes_narrow(1)
        regroup_g(2, 0, 96, 256, one)
        rope_store(0)
        one = gate(3)
        w_quant_both(2)
        passes_narrow(2)
        regroup_g(3, 0, 96, 256, one)
        rope_store(1)
        one = gate(4)
        w_quant_both(3)
        passes_narrow(3)
        regroup_g(4, 0, 96, 256, one)
        rope_store(2)
        one = gate(5)
        w_quant_both(4)
        passes_narrow(4)
        regroup_g(5, 0, 96, 256, one)
        rope_store(3)
        one = gate(6)
        w_quant_both(5)
        passes_narrow(5)
        regroup_g(6, 0, 96, 256, one)
        rope_store(4)
        one = gate(7)
        w_quant_both(6)
        passes_narrow(6)
        regroup_g(7, 0, 96, 256, one)
        rope_store(5)
        w_quant_both(7)
        passes_narrow(7)
        rope_store(6)
        rope_store(7)
